import numpy as np
import ml_dtypes


def mxq(x, axis, fmt="e4m3"):
    dtype, down = {"e4m3": (ml_dtypes.float8_e4m3fn, 7), "e5m2": (ml_dtypes.float8_e5m2, 14)}[fmt]
    v = np.moveaxis(np.asarray(x, np.float32).astype(ml_dtypes.bfloat16).astype(np.float64), axis, -1)
    blocks = v.reshape(v.shape[:-1] + (-1, 32))
    amax = np.abs(blocks).max(-1, keepdims=True)
    byte = np.maximum(np.where(amax > 0, np.frexp(amax)[1] - 1 + 127, 0) - down, 1)
    scale = np.exp2(byte - 127.0)
    codes = (blocks / scale).astype(np.float32).astype(dtype).astype(np.float64)
    return np.moveaxis((codes * scale).reshape(v.shape), -1, axis)


WIDE = False


def mx_kscale(k):
    if not WIDE:
        return np.ones(k)
    levels = np.array([10, -10, 5, -5, 0])
    if k % 512:
        return np.exp2(np.random.permutation(np.resize(levels, k // 32))).repeat(32)
    a = np.empty((k // 512, 16))
    for p in range(k // 512):
        a[p, :8] = np.random.permutation(np.resize(levels, 8))
        for g in range(8):
            far = levels[np.abs(levels - a[p, g]) >= 10]
            a[p, g + 8] = far[np.random.randint(len(far))]
    return np.exp2(a.ravel()).repeat(32)


BF16 = ml_dtypes.bfloat16


def bf(x):
    return np.asarray(x, np.float32).astype(BF16)


def f64(x):
    return np.asarray(x).astype(np.float64)


T, K, N = 1024, 1024, 4096
KK_THRESHOLD = 1e6


def setup_inputs():
    s = mx_kscale(K)
    r = s / s.max()
    return {"inputs": bf(np.random.standard_normal((T, K)) * 4.0 / np.sqrt(K) / r),
            "weight": bf(np.random.uniform(-1.0, 1.0, (N, K)) * r),
            "bias": bf(np.random.standard_normal(N) * 0.5),
            "nmk": bf(1.0 + 0.1 * np.random.standard_normal(1)),
            "kk": bf(1.0 + 0.1 * np.random.standard_normal(1))}


def reference(inputs, weight, bias, nmk, kk):
    kk_s = f64(kk)[0]
    w = f64(weight)
    w_bin = np.where(kk_s < KK_THRESHOLD, np.tanh(w * kk_s), np.sign(w))
    out = (mxq(f64(inputs), 1, "e4m3") @ mxq(w_bin, 1, "e4m3").T) + f64(bias)
    return f64(nmk)[0] * out

@@ -1,0 +1,221 @@
+from contextlib import ExitStack
+
+import concourse.mybir as mybir
+from concourse.masks import make_identity
+
+F32 = mybir.dt.float32
+BF16 = mybir.dt.bfloat16
+U32 = mybir.dt.uint32
+U8 = mybir.dt.uint8
+I32 = mybir.dt.int32
+FP8X4 = mybir.dt.float8_e4m3fn_x4
+ACT = mybir.ActivationFunctionType
+ALU = mybir.AluOpType
+
+P = 128
+T, K, N = 1024, 1024, 4096
+FLOPS = 2 * T * K * N
+NA = T // P
+CH = 512
+NCH = N // CH
+G = K // 512
+BIG = 3.4e38
+KK_THRESHOLD = 1.0e6
+PIN = True
+A_ST = 2
+OFFLOAD = []
+QH = (2, 5)
+QH0 = (5, 7)
+T1_AFTER = 1
+
+
+def tile_binarydense_kernel(tc, inputs, weight, bias, nmk, kk, out):
+    nc = tc.nc
+    with ExitStack() as ctx:
+        const = ctx.enter_context(tc.tile_pool(name="const", bufs=1))
+        wgp = ctx.enter_context(tc.tile_pool(name="wgp", bufs=2))
+        wcp = ctx.enter_context(tc.tile_pool(name="wcp", bufs=3))
+        osp = ctx.enter_context(tc.tile_pool(name="osp", bufs=12))
+        ps_t = ctx.enter_context(tc.psum_pool(name="ps_t", bufs=4))
+        ps_a = ctx.enter_context(tc.psum_pool(name="ps_a", bufs=4))
+        if PIN:
+            ctx.enter_context(tc.manual_schedule())
+
+        kk_bf = const.tile([P, 1], BF16, name="kk_bf")
+        nc.sync.dma_start(out=kk_bf[:], in_=kk.partition_broadcast(P))
+        nmk_bf = const.tile([P, 1], BF16, name="nmk_bf")
+        nc.scalar.dma_start(out=nmk_bf[:], in_=nmk.partition_broadcast(P))
+        brow = const.tile([P, CH], BF16, name="brow")
+        nc.vector.memset(brow[:].bitcast(I32), 0)
+        nc.scalar.dma_start(out=brow[0:NCH, :], in_=bias.rearrange("(c j) -> c j", c=NCH))
+
+        w_raw = []
+        for c in range(NCH):
+            w_raw.append(const.tile([P, 4 * K], BF16, name="w_raw%d" % c))
+        x_raw = const.tile([P, NA * K], BF16, name="x_raw")
+        x_src = inputs.rearrange("(p a) k -> p (a k)", a=NA)
+
+        def load_w(c, i, parts):
+            src = weight[c * CH:(c + 1) * CH, :].rearrange("(b p) k -> p b k", p=P)
+            nb = 4 // parts
+            nc.sync.dma_start(out=w_raw[c][:, i * nb * K:(i + 1) * nb * K].rearrange("p (b k) -> p b k", k=K),
+                              in_=src[:, i * nb:(i + 1) * nb, :])
+
+        def load_x(i):
+            nc.sync.dma_start(out=x_raw[:, i * 2048:(i + 1) * 2048], in_=x_src[:, i * 2048:(i + 1) * 2048])
+
+        load_w(0, 0, 2)
+        load_x(0)
+        load_w(0, 1, 2)
+        load_x(1)
+        load_x(2)
+        load_x(3)
+        for c in range(1, NCH):
+            load_w(c, 0, 1)
+
+        ident_f = const.tile([P, P], F32, name="ident_f")
+        make_identity(nc, ident_f[:])
+        ident_b = const.tile([P, P], BF16, name="ident_b")
+        make_identity(nc, ident_b[:])
+        kk_m = const.tile([P, 1], F32, name="kk_m")
+        nc.vector.tensor_scalar(out=kk_m[:], in0=kk_bf[:], scalar1=KK_THRESHOLD, scalar2=BIG,
+                                op0=ALU.is_ge, op1=ALU.mult)
+        kk_eff = const.tile([P, 1], F32, name="kk_eff")
+        nc.vector.tensor_scalar(out=kk_eff[:], in0=kk_bf[:], scalar1=kk_m[:, 0:1], scalar2=BIG,
+                                op0=ALU.add, op1=ALU.min)
+        nmk_f = const.tile([P, 1], F32, name="nmk_f")
+        nc.vector.tensor_copy(out=nmk_f[:], in_=nmk_bf[:])
+
+        bias_n = const.tile([P, N], F32, name="bias_n")
+        xg = const.tile([P, G, NA * 512], BF16, name="xg", align_bytes=64)
+        xc = const.tile([P, G, T], U32, name="xc", align_bytes=64)
+        xs = const.tile([P, G, T], U8, name="xs", align_bytes=64)
+        xgf = xg[:].bitcast(F32)
+        xf = x_raw[:].bitcast(F32)
+        out_v = out.rearrange("(r a) n -> r a n", a=NA)
+
+        wg_t = {}
+        wc_t = {}
+        ws_t = {}
+
+        def bias_chunk(c):
+            bp = ps_t.tile([P, CH], F32, name="bp", tag="tp")
+            nc.tensor.matmul(out=bp[:], lhsT=ident_b[:, c:c + 1].to_broadcast([P, P]), rhs=brow[:],
+                             start=True, stop=True)
+            nc.scalar.activation(out=bias_n[:, c * CH:(c + 1) * CH], in_=bp[:], func=ACT.Copy,
+                                 scale=nmk_f[:, 0:1])
+
+        def w_bank(c, g, bh):
+            wf = w_raw[c][:].bitcast(F32)
+            wg = wg_t[c]
+            tp = ps_t.tile([P, 512], F32, name="tp", tag="tp")
+            for m in range(4):
+                col = 512 * (2 * bh + m % 2) + 256 * g
+                nc.tensor.transpose(tp[:, 128 * m:128 * m + 128], wf[:, col + m // 2:col + 256:2], ident_f[:])
+            src = tp[:].bitcast(BF16).rearrange("p (u j e) -> p j u e", u=2, j=2 * P, e=2)
+            dst = wg[:, g, 1024 * bh:1024 * bh + 1024].rearrange("p (j u e) -> p j u e", j=2 * P, u=2, e=2)
+            nc.scalar.activation(out=dst, in_=src, func=ACT.Tanh, scale=kk_eff[:, 0:1])
+
+        def w_new(c):
+            wg_t[c] = wgp.tile([P, G, 4 * CH], BF16, name="wg", align_bytes=64)
+
+        def w_transpose(c):
+            w_new(c)
+            for g in range(G):
+                for bh in range(2):
+                    w_bank(c, g, bh)
+
+        def w_quant(c, g):
+            if g == 0:
+                wc_t[c] = wcp.tile([P, G, CH], U32, name="wc", align_bytes=64)
+                ws_t[c] = wcp.tile([P, G, CH], U8, name="ws", align_bytes=64)
+            nc.vector.quantize_mx(out=wc_t[c][:, g, :].bitcast(FP8X4), scales=ws_t[c][:, g, :],
+                                  in_=wg_t[c][:, g, :])
+
+        def x_transpose(a, eng):
+            tpx = ps_a.tile([P, 512], F32, name="tpx", tag="acc")
+            for j in range(4):
+                col = 512 * a + 256 * (j // 2)
+                nc.tensor.transpose(tpx[:, 128 * j:128 * j + 128], xf[:, col + j % 2:col + 256:2], ident_f[:])
+            dst = xgf[:, :, 256 * a:256 * a + 256].rearrange("p g (r u) -> p g r u", u=2)
+            src = tpx[:].rearrange("p (g u r) -> p g r u", g=G, u=2)
+            if eng == "v":
+                nc.vector.tensor_copy(out=dst, in_=src)
+            else:
+                nc.scalar.copy(out=dst, in_=src)
+
+        def x_quant(q):
+            for g in range(G):
+                nc.vector.quantize_mx(out=xc[:, g, 256 * q:256 * q + 256].bitcast(FP8X4),
+                                      scales=xs[:, g, 256 * q:256 * q + 256],
+                                      in_=xg[:, g, 1024 * q:1024 * q + 1024])
+
+        ost_t = {}
+
+        def mx_chunk(c, t_hooks, v_hooks):
+            wc = wc_t[c]
+            ws = ws_t[c]
+            cs = slice(c * CH, (c + 1) * CH)
+            for a in range(NA):
+                acc = ps_a.tile([P, CH], F32, name="acc", tag="acc")
+                for g in range(G):
+                    nc.tensor.matmul_mx(out=acc[:],
+                                        lhsT=xc[:, g, P * a:P * a + P].bitcast(FP8X4),
+                                        lhsT_scale=xs[:, g, P * a:P * a + P],
+                                        rhs=wc[:, g, :].bitcast(FP8X4),
+                                        rhs_scale=ws[:, g, :],
+                                        start=(g == 0), stop=(g == G - 1))
+                for f in t_hooks.get(a, []):
+                    f()
+                if a % A_ST == 0:
+                    ost_t[0] = osp.tile([P, A_ST, CH], F32, name="ost")
+                ost = ost_t[0]
+                if a in OFFLOAD and c < NCH - 1:
+                    nc.scalar.activation(out=ost[:, a % A_ST, :], in_=acc[:], func=ACT.Copy,
+                                         scale=nmk_f[:, 0:1])
+                    nc.gpsimd.tensor_tensor(out=ost[:, a % A_ST, :], in0=ost[:, a % A_ST, :],
+                                            in1=bias_n[:, cs], op=ALU.add)
+                else:
+                    nc.vector.scalar_tensor_tensor(out=ost[:, a % A_ST, :], in0=acc[:], scalar=nmk_f[:, 0:1],
+                                                   in1=bias_n[:, cs], op0=ALU.mult, op1=ALU.add)
+                if a % A_ST == A_ST - 1:
+                    nc.sync.dma_start(out=out_v[:, a - A_ST + 1:a + 1, cs], in_=ost[:])
+                for f in v_hooks.get(a, []):
+                    f()
+
+        w_new(0)
+        w_bank(0, 0, 0)
+        w_bank(0, 1, 0)
+        x_transpose(0, "v")
+        x_transpose(1, "v")
+        x_quant(0)
+        w_bank(0, 0, 1)
+        w_bank(0, 1, 1)
+        bias_chunk(0)
+        x_transpose(2, "v")
+        x_transpose(3, "v")
+        x_quant(1)
+        for a in range(4, NA):
+            x_transpose(a, "s")
+        w_quant(0, 0)
+        w_quant(0, 1)
+        x_quant(2)
+
+        def t_run(c):
+            bias_chunk(c)
+            w_transpose(c)
+
+        for c in range(NCH):
+            t_hooks = {}
+            v_hooks = {}
+            if c == 0:
+                t_hooks[T1_AFTER] = [lambda: t_run(1)]
+                v_hooks[0] = [lambda: x_quant(3)]
+                v_hooks[QH0[0]] = [lambda: w_quant(1, 0)]
+                v_hooks[QH0[1]] = [lambda: w_quant(1, 1)]
+            elif c + 1 < NCH:
+                n = c + 1
+                v_hooks[QH[0]] = [lambda: w_quant(n, 0)]
+                v_hooks[QH[1]] = [lambda: w_quant(n, 1)]
+                t_run(n)
+            mx_chunk(c, t_hooks, v_hooks)

@@ -21,12 +21,7 @@ NCH = N // CH
 G = K // 512
 BIG = 3.4e38
 KK_THRESHOLD = 1.0e6
-PIN = True
-A_ST = 2
-OFFLOAD = []
-QH = (2, 5)
-QH0 = (5, 7)
-T1_AFTER = 1
+PERMUTE = (2, 3)
 
 
 def tile_binarydense_kernel(tc, inputs, weight, bias, nmk, kk, out):
@@ -35,19 +30,23 @@ def tile_binarydense_kernel(tc, inputs, weight, bias, nmk, kk, out):
         const = ctx.enter_context(tc.tile_pool(name="const", bufs=1))
         wgp = ctx.enter_context(tc.tile_pool(name="wgp", bufs=2))
         wcp = ctx.enter_context(tc.tile_pool(name="wcp", bufs=3))
-        osp = ctx.enter_context(tc.tile_pool(name="osp", bufs=12))
+        osp = ctx.enter_context(tc.tile_pool(name="osp", bufs=10))
+        wpp = ctx.enter_context(tc.tile_pool(name="wpp", bufs=2))
         ps_t = ctx.enter_context(tc.psum_pool(name="ps_t", bufs=4))
         ps_a = ctx.enter_context(tc.psum_pool(name="ps_a", bufs=4))
-        if PIN:
-            ctx.enter_context(tc.manual_schedule())
+        ctx.enter_context(tc.manual_schedule())
 
-        kk_bf = const.tile([P, 1], BF16, name="kk_bf")
-        nc.sync.dma_start(out=kk_bf[:], in_=kk.partition_broadcast(P))
-        nmk_bf = const.tile([P, 1], BF16, name="nmk_bf")
-        nc.scalar.dma_start(out=nmk_bf[:], in_=nmk.partition_broadcast(P))
         brow = const.tile([P, CH], BF16, name="brow")
         nc.vector.memset(brow[:].bitcast(I32), 0)
-        nc.scalar.dma_start(out=brow[0:NCH, :], in_=bias.rearrange("(c j) -> c j", c=NCH))
+        zero = const.tile([P, 1], F32, name="zero")
+        nc.vector.memset(zero[:], 0.0)
+        nc.sync.dma_start(out=brow[0:NCH, :], in_=bias.rearrange("(c j) -> c j", c=NCH))
+        kk_bf = const.tile([P, 1], BF16, name="kk_bf")
+        nc.scalar.dma_start(out=kk_bf[:], in_=kk.partition_broadcast(P))
+        nmk_bf = const.tile([P, 1], BF16, name="nmk_bf")
+        nc.scalar.dma_start(out=nmk_bf[:], in_=nmk.partition_broadcast(P))
+        warm = const.tile([P, 1], F32, name="warm")
+        nc.scalar.activation(out=warm[:], in_=zero[:], func=ACT.Tanh)
 
         w_raw = []
         for c in range(NCH):
@@ -55,28 +54,29 @@ def tile_binarydense_kernel(tc, inputs, weight, bias, nmk, kk, out):
         x_raw = const.tile([P, NA * K], BF16, name="x_raw")
         x_src = inputs.rearrange("(p a) k -> p (a k)", a=NA)
 
-        def load_w(c, i, parts):
-            src = weight[c * CH:(c + 1) * CH, :].rearrange("(b p) k -> p b k", p=P)
-            nb = 4 // parts
-            nc.sync.dma_start(out=w_raw[c][:, i * nb * K:(i + 1) * nb * K].rearrange("p (b k) -> p b k", k=K),
-                              in_=src[:, i * nb:(i + 1) * nb, :])
+        def load_w(c, h0, h1):
+            src = weight[c * CH:(c + 1) * CH, :].rearrange("(h p b) k -> p h (b k)", h=2, b=2)
+            nc.sync.dma_start(out=w_raw[c][:, 2048 * h0:2048 * h1].rearrange("p (h x) -> p h x", x=2 * K),
+                              in_=src[:, h0:h1, :])
 
         def load_x(i):
             nc.sync.dma_start(out=x_raw[:, i * 2048:(i + 1) * 2048], in_=x_src[:, i * 2048:(i + 1) * 2048])
 
-        load_w(0, 0, 2)
+        load_w(0, 0, 1)
         load_x(0)
         load_w(0, 1, 2)
         load_x(1)
+        load_w(1, 0, 1)
         load_x(2)
         load_x(3)
-        for c in range(1, NCH):
-            load_w(c, 0, 1)
+        load_w(1, 1, 2)
+        for c in range(2, NCH):
+            load_w(c, 0, 2)
 
-        ident_f = const.tile([P, P], F32, name="ident_f")
-        make_identity(nc, ident_f[:])
         ident_b = const.tile([P, P], BF16, name="ident_b")
         make_identity(nc, ident_b[:])
+        ident_f = const.tile([P, P], F32, name="ident_f")
+        make_identity(nc, ident_f[:])
         kk_m = const.tile([P, 1], F32, name="kk_m")
         nc.vector.tensor_scalar(out=kk_m[:], in0=kk_bf[:], scalar1=KK_THRESHOLD, scalar2=BIG,
                                 op0=ALU.is_ge, op1=ALU.mult)
@@ -94,36 +94,50 @@ def tile_binarydense_kernel(tc, inputs, weight, bias, nmk, kk, out):
         xf = x_raw[:].bitcast(F32)
         out_v = out.rearrange("(r a) n -> r a n", a=NA)
 
+        wp_t = {}
         wg_t = {}
         wc_t = {}
         ws_t = {}
+        acc_t = {}
+        ost_t = {}
 
-        def bias_chunk(c):
+        def w_permute(c):
+            wp_t[c] = wpp.tile([P, 4 * 512], F32, name="wp")
+            for m in PERMUTE:
+                cols = slice(512 * m, 512 * m + 512)
+                nc.scalar.copy(
+                    out=wp_t[c][:, cols].rearrange("p (g u w) -> p g u w", g=G, u=2),
+                    in_=w_raw[c][:].bitcast(F32)[:, cols].rearrange("p (g w u) -> p g u w", g=G, u=2))
+
+        def bias_chunk(c, eng):
             bp = ps_t.tile([P, CH], F32, name="bp", tag="tp")
             nc.tensor.matmul(out=bp[:], lhsT=ident_b[:, c:c + 1].to_broadcast([P, P]), rhs=brow[:],
                              start=True, stop=True)
-            nc.scalar.activation(out=bias_n[:, c * CH:(c + 1) * CH], in_=bp[:], func=ACT.Copy,
-                                 scale=nmk_f[:, 0:1])
+            dst = bias_n[:, c * CH:(c + 1) * CH]
+            if eng == "v":
+                nc.vector.tensor_scalar(out=dst, in0=bp[:], scalar1=nmk_f[:, 0:1], scalar2=None, op0=ALU.mult)
+            else:
+                nc.scalar.activation(out=dst, in_=bp[:], func=ACT.Copy, scale=nmk_f[:, 0:1])
 
         def w_bank(c, g, bh):
-            wf = w_raw[c][:].bitcast(F32)
             wg = wg_t[c]
             tp = ps_t.tile([P, 512], F32, name="tp", tag="tp")
             for m in range(4):
-                col = 512 * (2 * bh + m % 2) + 256 * g
-                nc.tensor.transpose(tp[:, 128 * m:128 * m + 128], wf[:, col + m // 2:col + 256:2], ident_f[:])
+                blk = 2 * bh + m % 2
+                col = 512 * blk + 256 * g
+                u = m // 2
+                if c in wp_t and blk in PERMUTE:
+                    words = wp_t[c][:, col + 128 * u:col + 128 * u + 128]
+                else:
+                    words = w_raw[c][:].bitcast(F32)[:, col + u:col + 256:2]
+                nc.tensor.transpose(tp[:, 128 * m:128 * m + 128], words, ident_f[:])
             src = tp[:].bitcast(BF16).rearrange("p (u j e) -> p j u e", u=2, j=2 * P, e=2)
-            dst = wg[:, g, 1024 * bh:1024 * bh + 1024].rearrange("p (j u e) -> p j u e", j=2 * P, u=2, e=2)
+            src = src.rearrange("p (b j) u e -> p b j u e", b=2)
+            dst = wg[:, g, :].rearrange("p (b h j u e) -> p h b j u e", b=2, h=2, j=P, u=2, e=2)[:, bh]
             nc.scalar.activation(out=dst, in_=src, func=ACT.Tanh, scale=kk_eff[:, 0:1])
 
         def w_new(c):
             wg_t[c] = wgp.tile([P, G, 4 * CH], BF16, name="wg", align_bytes=64)
-
-        def w_transpose(c):
-            w_new(c)
-            for g in range(G):
-                for bh in range(2):
-                    w_bank(c, g, bh)
 
         def w_quant(c, g):
             if g == 0:
@@ -132,17 +146,14 @@ def tile_binarydense_kernel(tc, inputs, weight, bias, nmk, kk, out):
             nc.vector.quantize_mx(out=wc_t[c][:, g, :].bitcast(FP8X4), scales=ws_t[c][:, g, :],
                                   in_=wg_t[c][:, g, :])
 
-        def x_transpose(a, eng):
+        def x_transpose(a):
             tpx = ps_a.tile([P, 512], F32, name="tpx", tag="acc")
             for j in range(4):
                 col = 512 * a + 256 * (j // 2)
                 nc.tensor.transpose(tpx[:, 128 * j:128 * j + 128], xf[:, col + j % 2:col + 256:2], ident_f[:])
             dst = xgf[:, :, 256 * a:256 * a + 256].rearrange("p g (r u) -> p g r u", u=2)
             src = tpx[:].rearrange("p (g u r) -> p g r u", g=G, u=2)
-            if eng == "v":
-                nc.vector.tensor_copy(out=dst, in_=src)
-            else:
-                nc.scalar.copy(out=dst, in_=src)
+            nc.vector.tensor_copy(out=dst, in_=src)
 
         def x_quant(q):
             for g in range(G):
@@ -150,72 +161,88 @@ def tile_binarydense_kernel(tc, inputs, weight, bias, nmk, kk, out):
                                       scales=xs[:, g, 256 * q:256 * q + 256],
                                       in_=xg[:, g, 1024 * q:1024 * q + 1024])
 
-        ost_t = {}
+        def mx(c, a):
+            acc = ps_a.tile([P, CH], F32, name="acc", tag="acc")
+            for g in range(G):
+                nc.tensor.matmul_mx(out=acc[:],
+                                    lhsT=xc[:, g, P * a:P * a + P].bitcast(FP8X4),
+                                    lhsT_scale=xs[:, g, P * a:P * a + P],
+                                    rhs=wc_t[c][:, g, :].bitcast(FP8X4),
+                                    rhs_scale=ws_t[c][:, g, :],
+                                    start=(g == 0), stop=(g == G - 1))
+            acc_t[a] = acc
 
-        def mx_chunk(c, t_hooks, v_hooks):
-            wc = wc_t[c]
-            ws = ws_t[c]
+        def epilogue(c, a):
+            n_st = 1 if c == NCH - 1 else 2
             cs = slice(c * CH, (c + 1) * CH)
-            for a in range(NA):
-                acc = ps_a.tile([P, CH], F32, name="acc", tag="acc")
-                for g in range(G):
-                    nc.tensor.matmul_mx(out=acc[:],
-                                        lhsT=xc[:, g, P * a:P * a + P].bitcast(FP8X4),
-                                        lhsT_scale=xs[:, g, P * a:P * a + P],
-                                        rhs=wc[:, g, :].bitcast(FP8X4),
-                                        rhs_scale=ws[:, g, :],
-                                        start=(g == 0), stop=(g == G - 1))
-                for f in t_hooks.get(a, []):
-                    f()
-                if a % A_ST == 0:
-                    ost_t[0] = osp.tile([P, A_ST, CH], F32, name="ost")
-                ost = ost_t[0]
-                if a in OFFLOAD and c < NCH - 1:
-                    nc.scalar.activation(out=ost[:, a % A_ST, :], in_=acc[:], func=ACT.Copy,
-                                         scale=nmk_f[:, 0:1])
-                    nc.gpsimd.tensor_tensor(out=ost[:, a % A_ST, :], in0=ost[:, a % A_ST, :],
-                                            in1=bias_n[:, cs], op=ALU.add)
-                else:
-                    nc.vector.scalar_tensor_tensor(out=ost[:, a % A_ST, :], in0=acc[:], scalar=nmk_f[:, 0:1],
-                                                   in1=bias_n[:, cs], op0=ALU.mult, op1=ALU.add)
-                if a % A_ST == A_ST - 1:
-                    nc.sync.dma_start(out=out_v[:, a - A_ST + 1:a + 1, cs], in_=ost[:])
-                for f in v_hooks.get(a, []):
-                    f()
+            if a % n_st == 0:
+                ost_t[0] = osp.tile([P, 2, CH], F32, name="ost")
+            ost = ost_t[0]
+            nc.vector.scalar_tensor_tensor(
+                out=ost[:, a % n_st, :].rearrange("q (j b) -> q j b", b=2),
+                in0=acc_t[a][:].rearrange("q (b j) -> q j b", b=2), scalar=nmk_f[:, 0:1],
+                in1=bias_n[:, cs].rearrange("q (j b) -> q j b", b=2), op0=ALU.mult, op1=ALU.add)
+            if a % n_st == n_st - 1:
+                nc.sync.dma_start(out=out_v[:, a - n_st + 1:a + 1, cs], in_=ost[:, 0:n_st, :])
 
+        bias_chunk(0, "v")
+        bias_chunk(1, "v")
         w_new(0)
         w_bank(0, 0, 0)
         w_bank(0, 1, 0)
-        x_transpose(0, "v")
-        x_transpose(1, "v")
-        x_quant(0)
+        bias_chunk(2, "v")
+        x_transpose(0)
+        x_transpose(1)
         w_bank(0, 0, 1)
         w_bank(0, 1, 1)
-        bias_chunk(0)
-        x_transpose(2, "v")
-        x_transpose(3, "v")
-        x_quant(1)
-        for a in range(4, NA):
-            x_transpose(a, "s")
+        x_quant(0)
+        bias_chunk(3, "v")
+        x_transpose(2)
         w_quant(0, 0)
+        x_transpose(3)
         w_quant(0, 1)
+        x_quant(1)
+        w_new(1)
+        w_bank(1, 0, 0)
+        w_bank(1, 1, 0)
+        x_transpose(4)
+        x_transpose(5)
+        mx(0, 0)
+        epilogue(0, 0)
         x_quant(2)
+        mx(0, 1)
+        epilogue(0, 1)
+        x_transpose(6)
+        x_transpose(7)
+        w_bank(1, 0, 1)
+        w_bank(1, 1, 1)
+        mx(0, 2)
+        epilogue(0, 2)
+        x_quant(3)
+        for a in range(3, NA):
+            mx(0, a)
+            epilogue(0, a)
+            if a == 4:
+                w_quant(1, 0)
+            if a == 6:
+                w_quant(1, 1)
+        w_permute(2)
 
-        def t_run(c):
-            bias_chunk(c)
-            w_transpose(c)
-
-        for c in range(NCH):
-            t_hooks = {}
-            v_hooks = {}
-            if c == 0:
-                t_hooks[T1_AFTER] = [lambda: t_run(1)]
-                v_hooks[0] = [lambda: x_quant(3)]
-                v_hooks[QH0[0]] = [lambda: w_quant(1, 0)]
-                v_hooks[QH0[1]] = [lambda: w_quant(1, 1)]
-            elif c + 1 < NCH:
-                n = c + 1
-                v_hooks[QH[0]] = [lambda: w_quant(n, 0)]
-                v_hooks[QH[1]] = [lambda: w_quant(n, 1)]
-                t_run(n)
-            mx_chunk(c, t_hooks, v_hooks)
+        for c in range(1, NCH):
+            n = c + 1
+            if n < NCH:
+                w_new(n)
+                for g in range(G):
+                    for bh in range(2):
+                        w_bank(n, g, bh)
+            for a in range(NA):
+                mx(c, a)
+                if a == 3 and c + 3 < NCH:
+                    bias_chunk(c + 3, "s")
+                epilogue(c, a)
+                if n < NCH and a == 2:
+                    w_quant(n, 0)
+                if n < NCH and a == 5:
+                    w_quant(n, 1)
+            if n + 1 < NCH:
+                w_permute(n + 1)

@@ -21,7 +21,7 @@ NCH = N // CH
 G = K // 512
 BIG = 3.4e38
 KK_THRESHOLD = 1.0e6
-PERMUTE = (2, 3)
+PERMUTE = {1: "s", 2: "s", 3: "s"}
 
 
 def tile_binarydense_kernel(tc, inputs, weight, bias, nmk, kk, out):
@@ -101,13 +101,19 @@ def tile_binarydense_kernel(tc, inputs, weight, bias, nmk, kk, out):
         acc_t = {}
         ost_t = {}
 
-        def w_permute(c):
-            wp_t[c] = wpp.tile([P, 4 * 512], F32, name="wp")
-            for m in PERMUTE:
+        def w_permute(c, eng):
+            if c not in wp_t:
+                wp_t[c] = wpp.tile([P, 4 * 512], F32, name="wp")
+            for m in range(4):
+                if PERMUTE.get(m) != eng:
+                    continue
                 cols = slice(512 * m, 512 * m + 512)
-                nc.scalar.copy(
-                    out=wp_t[c][:, cols].rearrange("p (g u w) -> p g u w", g=G, u=2),
-                    in_=w_raw[c][:].bitcast(F32)[:, cols].rearrange("p (g w u) -> p g u w", g=G, u=2))
+                dst = wp_t[c][:, cols].rearrange("p (g u w) -> p g u w", g=G, u=2)
+                src = w_raw[c][:].bitcast(F32)[:, cols].rearrange("p (g w u) -> p g u w", g=G, u=2)
+                if eng == "s":
+                    nc.scalar.copy(out=dst, in_=src)
+                else:
+                    nc.vector.tensor_copy(out=dst, in_=src)
 
         def bias_chunk(c, eng):
             bp = ps_t.tile([P, CH], F32, name="bp", tag="tp")
@@ -146,14 +152,17 @@ def tile_binarydense_kernel(tc, inputs, weight, bias, nmk, kk, out):
             nc.vector.quantize_mx(out=wc_t[c][:, g, :].bitcast(FP8X4), scales=ws_t[c][:, g, :],
                                   in_=wg_t[c][:, g, :])
 
-        def x_transpose(a):
+        def x_transpose(a, eng="v"):
             tpx = ps_a.tile([P, 512], F32, name="tpx", tag="acc")
             for j in range(4):
                 col = 512 * a + 256 * (j // 2)
                 nc.tensor.transpose(tpx[:, 128 * j:128 * j + 128], xf[:, col + j % 2:col + 256:2], ident_f[:])
             dst = xgf[:, :, 256 * a:256 * a + 256].rearrange("p g (r u) -> p g r u", u=2)
             src = tpx[:].rearrange("p (g u r) -> p g r u", g=G, u=2)
-            nc.vector.tensor_copy(out=dst, in_=src)
+            if eng == "v":
+                nc.vector.tensor_copy(out=dst, in_=src)
+            else:
+                nc.scalar.copy(out=dst, in_=src)
 
         def x_quant(q):
             for g in range(G):
@@ -190,13 +199,11 @@ def tile_binarydense_kernel(tc, inputs, weight, bias, nmk, kk, out):
         w_new(0)
         w_bank(0, 0, 0)
         w_bank(0, 1, 0)
-        bias_chunk(2, "v")
         x_transpose(0)
         x_transpose(1)
         w_bank(0, 0, 1)
         w_bank(0, 1, 1)
         x_quant(0)
-        bias_chunk(3, "v")
         x_transpose(2)
         w_quant(0, 0)
         x_transpose(3)
@@ -207,42 +214,50 @@ def tile_binarydense_kernel(tc, inputs, weight, bias, nmk, kk, out):
         w_bank(1, 1, 0)
         x_transpose(4)
         x_transpose(5)
+        bias_chunk(2, "s")
+        bias_chunk(3, "s")
         mx(0, 0)
         epilogue(0, 0)
         x_quant(2)
         mx(0, 1)
         epilogue(0, 1)
-        x_transpose(6)
-        x_transpose(7)
-        w_bank(1, 0, 1)
-        w_bank(1, 1, 1)
+        x_transpose(6, "s")
+        x_transpose(7, "s")
         mx(0, 2)
         epilogue(0, 2)
         x_quant(3)
+        w_bank(1, 0, 1)
+        w_bank(1, 1, 1)
         for a in range(3, NA):
             mx(0, a)
             epilogue(0, a)
+            if a == 3:
+                w_permute(2, "v")
             if a == 4:
                 w_quant(1, 0)
             if a == 6:
                 w_quant(1, 1)
-        w_permute(2)
+        w_permute(2, "s")
 
         for c in range(1, NCH):
             n = c + 1
             if n < NCH:
                 w_new(n)
+                k = 0
                 for g in range(G):
                     for bh in range(2):
                         w_bank(n, g, bh)
+                        k += 1
+                        if k == 2 and n + 1 < NCH:
+                            w_permute(n + 1, "s")
             for a in range(NA):
                 mx(c, a)
                 if a == 3 and c + 3 < NCH:
                     bias_chunk(c + 3, "s")
                 epilogue(c, a)
+                if n + 1 < NCH and a == 0:
+                    w_permute(n + 1, "v")
                 if n < NCH and a == 2:
                     w_quant(n, 0)
-                if n < NCH and a == 5:
+                if n < NCH and a == (6 if n < NCH - 1 else 5):
                     w_quant(n, 1)
-            if n + 1 < NCH:
-                w_permute(n + 1)

@@ -70,8 +70,11 @@ def tile_binarydense_kernel(tc, inputs, weight, bias, nmk, kk, out):
         load_x(2)
         load_x(3)
         load_w(1, 1, 2)
+        bias_b = const.tile([P, N - 2 * CH], BF16, name="bias_b")
         for c in range(2, NCH):
             load_w(c, 0, 2)
+            if c == 5:
+                nc.sync.dma_start(out=bias_b[:], in_=bias[2 * CH:N].partition_broadcast(P))
 
         ident_b = const.tile([P, P], BF16, name="ident_b")
         make_identity(nc, ident_b[:])
@@ -124,6 +127,11 @@ def tile_binarydense_kernel(tc, inputs, weight, bias, nmk, kk, out):
                 nc.vector.tensor_scalar(out=dst, in0=bp[:], scalar1=nmk_f[:, 0:1], scalar2=None, op0=ALU.mult)
             else:
                 nc.scalar.activation(out=dst, in_=bp[:], func=ACT.Copy, scale=nmk_f[:, 0:1])
+
+        def bias_scale(c):
+            cs = slice(c * CH, (c + 1) * CH)
+            nc.gpsimd.tensor_scalar(out=bias_n[:, cs], in0=bias_b[:, (c - 2) * CH:(c - 1) * CH], scalar1=nmk_f[:, 0:1],
+                                    scalar2=0.0, op0=ALU.mult, op1=ALU.add)
 
         def w_bank(c, g, bh):
             wg = wg_t[c]
@@ -214,8 +222,6 @@ def tile_binarydense_kernel(tc, inputs, weight, bias, nmk, kk, out):
         w_bank(1, 1, 0)
         x_transpose(4)
         x_transpose(5)
-        bias_chunk(2, "s")
-        bias_chunk(3, "s")
         mx(0, 0)
         epilogue(0, 0)
         x_quant(2)
@@ -252,8 +258,8 @@ def tile_binarydense_kernel(tc, inputs, weight, bias, nmk, kk, out):
                             w_permute(n + 1, "s")
             for a in range(NA):
                 mx(c, a)
-                if a == 3 and c + 3 < NCH:
-                    bias_chunk(c + 3, "s")
+                if a == 3 and n < NCH:
+                    bias_scale(n)
                 epilogue(c, a)
                 if n + 1 < NCH and a == 0:
                     w_permute(n + 1, "v")

@@ -66,8 +66,8 @@ def tile_binarydense_kernel(tc, inputs, weight, bias, nmk, kk, out):
         load_x(0)
         load_w(0, 1, 2)
         load_x(1)
-        load_w(1, 0, 1)
         load_x(2)
+        load_w(1, 0, 1)
         load_x(3)
         load_w(1, 1, 2)
         bias_b = const.tile([P, N - 2 * CH], BF16, name="bias_b")
@@ -90,10 +90,13 @@ def tile_binarydense_kernel(tc, inputs, weight, bias, nmk, kk, out):
         nc.vector.tensor_copy(out=nmk_f[:], in_=nmk_bf[:])
 
         bias_n = const.tile([P, N], F32, name="bias_n")
-        xg = const.tile([P, G, NA * 512], BF16, name="xg", align_bytes=64)
-        xc = const.tile([P, G, T], U32, name="xc", align_bytes=64)
-        xs = const.tile([P, G, T], U8, name="xs", align_bytes=64)
-        xgf = xg[:].bitcast(F32)
+        xg = []
+        xc = []
+        xs = []
+        for q in range(NA // 2):
+            xg.append(const.tile([P, G, 1024], BF16, name="xg%d" % q, align_bytes=64))
+            xc.append(const.tile([P, G, 256], U32, name="xc%d" % q, align_bytes=64))
+            xs.append(const.tile([P, G, 256], U8, name="xs%d" % q, align_bytes=64))
         xf = x_raw[:].bitcast(F32)
         out_v = out.rearrange("(r a) n -> r a n", a=NA)
 
@@ -165,7 +168,8 @@ def tile_binarydense_kernel(tc, inputs, weight, bias, nmk, kk, out):
             for j in range(4):
                 col = 512 * a + 256 * (j // 2)
                 nc.tensor.transpose(tpx[:, 128 * j:128 * j + 128], xf[:, col + j % 2:col + 256:2], ident_f[:])
-            dst = xgf[:, :, 256 * a:256 * a + 256].rearrange("p g (r u) -> p g r u", u=2)
+            r0 = 256 * (a % 2)
+            dst = xg[a // 2][:].bitcast(F32)[:, :, r0:r0 + 256].rearrange("p g (r u) -> p g r u", u=2)
             src = tpx[:].rearrange("p (g u r) -> p g r u", g=G, u=2)
             if eng == "v":
                 nc.vector.tensor_copy(out=dst, in_=src)
@@ -173,24 +177,23 @@ def tile_binarydense_kernel(tc, inputs, weight, bias, nmk, kk, out):
                 nc.scalar.copy(out=dst, in_=src)
 
         def x_quant(q):
-            for g in range(G):
-                nc.vector.quantize_mx(out=xc[:, g, 256 * q:256 * q + 256].bitcast(FP8X4),
-                                      scales=xs[:, g, 256 * q:256 * q + 256],
-                                      in_=xg[:, g, 1024 * q:1024 * q + 1024])
+            nc.vector.quantize_mx(out=xc[q][:].rearrange("p g t -> p (g t)").bitcast(FP8X4),
+                                  scales=xs[q][:].rearrange("p g t -> p (g t)"),
+                                  in_=xg[q][:].rearrange("p g t -> p (g t)"))
 
         def mx(c, a):
             acc = ps_a.tile([P, CH], F32, name="acc", tag="acc")
             for g in range(G):
                 nc.tensor.matmul_mx(out=acc[:],
-                                    lhsT=xc[:, g, P * a:P * a + P].bitcast(FP8X4),
-                                    lhsT_scale=xs[:, g, P * a:P * a + P],
+                                    lhsT=xc[a // 2][:, g, P * (a % 2):P * (a % 2) + P].bitcast(FP8X4),
+                                    lhsT_scale=xs[a // 2][:, g, P * (a % 2):P * (a % 2) + P],
                                     rhs=wc_t[c][:, g, :].bitcast(FP8X4),
                                     rhs_scale=ws_t[c][:, g, :],
                                     start=(g == 0), stop=(g == G - 1))
             acc_t[a] = acc
 
         def epilogue(c, a):
-            n_st = 1 if c == NCH - 1 else 2
+            n_st = 1 if c >= NCH - 2 else 2
             cs = slice(c * CH, (c + 1) * CH)
             if a % n_st == 0:
                 ost_t[0] = osp.tile([P, 2, CH], F32, name="ost")
@@ -217,11 +220,11 @@ def tile_binarydense_kernel(tc, inputs, weight, bias, nmk, kk, out):
         x_transpose(3)
         w_quant(0, 1)
         x_quant(1)
+        x_transpose(4, "s")
+        x_transpose(5, "s")
         w_new(1)
         w_bank(1, 0, 0)
         w_bank(1, 1, 0)
-        x_transpose(4)
-        x_transpose(5)
         mx(0, 0)
         epilogue(0, 0)
         x_quant(2)
@@ -265,5 +268,5 @@ def tile_binarydense_kernel(tc, inputs, weight, bias, nmk, kk, out):
                     w_permute(n + 1, "v")
                 if n < NCH and a == 2:
                     w_quant(n, 0)
-                if n < NCH and a == (6 if n < NCH - 1 else 5):
+                if n < NCH and a == (6 if n < NCH - 1 else 4):
                     w_quant(n, 1)

@@ -21,7 +21,7 @@ NCH = N // CH
 G = K // 512
 BIG = 3.4e38
 KK_THRESHOLD = 1.0e6
-PERMUTE = {1: "s", 2: "s", 3: "s"}
+PERMUTE = {0: "g", 1: "s", 2: "s", 3: "s"}
 
 
 def tile_binarydense_kernel(tc, inputs, weight, bias, nmk, kk, out):
@@ -31,7 +31,7 @@ def tile_binarydense_kernel(tc, inputs, weight, bias, nmk, kk, out):
         wgp = ctx.enter_context(tc.tile_pool(name="wgp", bufs=2))
         wcp = ctx.enter_context(tc.tile_pool(name="wcp", bufs=3))
         osp = ctx.enter_context(tc.tile_pool(name="osp", bufs=10))
-        wpp = ctx.enter_context(tc.tile_pool(name="wpp", bufs=2))
+        wpp = ctx.enter_context(tc.tile_pool(name="wpp", bufs=3))
         ps_t = ctx.enter_context(tc.psum_pool(name="ps_t", bufs=4))
         ps_a = ctx.enter_context(tc.psum_pool(name="ps_a", bufs=4))
         ctx.enter_context(tc.manual_schedule())
@@ -73,7 +73,7 @@ def tile_binarydense_kernel(tc, inputs, weight, bias, nmk, kk, out):
         bias_b = const.tile([P, N - 2 * CH], BF16, name="bias_b")
         for c in range(2, NCH):
             load_w(c, 0, 2)
-            if c == 5:
+            if c == 4:
                 nc.sync.dma_start(out=bias_b[:], in_=bias[2 * CH:N].partition_broadcast(P))
 
         ident_b = const.tile([P, P], BF16, name="ident_b")
@@ -118,6 +118,13 @@ def tile_binarydense_kernel(tc, inputs, weight, bias, nmk, kk, out):
                 src = w_raw[c][:].bitcast(F32)[:, cols].rearrange("p (g w u) -> p g u w", g=G, u=2)
                 if eng == "s":
                     nc.scalar.copy(out=dst, in_=src)
+                elif eng == "g":
+                    for g in range(G):
+                        gs = slice(512 * m + 256 * g, 512 * m + 256 * g + 256)
+                        nc.gpsimd.tensor_scalar(
+                            out=wp_t[c][:, gs].bitcast(BF16).rearrange("p (u w e) -> p u w e", u=2, e=2),
+                            in0=w_raw[c][:].bitcast(F32)[:, gs].bitcast(BF16).rearrange("p (w u e) -> p u w e", u=2, e=2),
+                            scalar1=1.0, scalar2=0.0, op0=ALU.mult, op1=ALU.add)
                 else:
                     nc.vector.tensor_copy(out=dst, in_=src)
 
@@ -248,6 +255,8 @@ def tile_binarydense_kernel(tc, inputs, weight, bias, nmk, kk, out):
                 w_quant(1, 1)
         w_permute(2, "s")
 
+        w_permute(2, "g")
+        w_permute(3, "g")
         for c in range(1, NCH):
             n = c + 1
             if n < NCH:
@@ -263,6 +272,8 @@ def tile_binarydense_kernel(tc, inputs, weight, bias, nmk, kk, out):
                 mx(c, a)
                 if a == 3 and n < NCH:
                     bias_scale(n)
+                if a == 3 and c + 3 < NCH:
+                    w_permute(c + 3, "g")
                 epilogue(c, a)
                 if n + 1 < NCH and a == 0:
                     w_permute(n + 1, "v")

from contextlib import ExitStack

import concourse.mybir as mybir
from concourse.masks import make_identity

F32 = mybir.dt.float32
BF16 = mybir.dt.bfloat16
U32 = mybir.dt.uint32
U8 = mybir.dt.uint8
I32 = mybir.dt.int32
FP8X4 = mybir.dt.float8_e4m3fn_x4
ACT = mybir.ActivationFunctionType
ALU = mybir.AluOpType

P = 128
T, K, N = 1024, 1024, 4096
FLOPS = 2 * T * K * N
NA = T // P
CH = 512
NCH = N // CH
G = K // 512
BIG = 3.4e38
KK_THRESHOLD = 1.0e6
PERMUTE = {0: "g", 1: "s", 2: "s", 3: "s"}


def tile_binarydense_kernel(tc, inputs, weight, bias, nmk, kk, out):
    nc = tc.nc
    with ExitStack() as ctx:
        const = ctx.enter_context(tc.tile_pool(name="const", bufs=1))
        wgp = ctx.enter_context(tc.tile_pool(name="wgp", bufs=2))
        wcp = ctx.enter_context(tc.tile_pool(name="wcp", bufs=3))
        osp = ctx.enter_context(tc.tile_pool(name="osp", bufs=10))
        wpp = ctx.enter_context(tc.tile_pool(name="wpp", bufs=3))
        ps_t = ctx.enter_context(tc.psum_pool(name="ps_t", bufs=4))
        ps_a = ctx.enter_context(tc.psum_pool(name="ps_a", bufs=4))
        ctx.enter_context(tc.manual_schedule())

        brow = const.tile([P, CH], BF16, name="brow")
        nc.vector.memset(brow[:].bitcast(I32), 0)
        zero = const.tile([P, 1], F32, name="zero")
        nc.vector.memset(zero[:], 0.0)
        nc.sync.dma_start(out=brow[0:NCH, :], in_=bias.rearrange("(c j) -> c j", c=NCH))
        kk_bf = const.tile([P, 1], BF16, name="kk_bf")
        nc.scalar.dma_start(out=kk_bf[:], in_=kk.partition_broadcast(P))
        nmk_bf = const.tile([P, 1], BF16, name="nmk_bf")
        nc.scalar.dma_start(out=nmk_bf[:], in_=nmk.partition_broadcast(P))
        warm = const.tile([P, 1], F32, name="warm")
        nc.scalar.activation(out=warm[:], in_=zero[:], func=ACT.Tanh)

        w_raw = []
        for c in range(NCH):
            w_raw.append(const.tile([P, 4 * K], BF16, name="w_raw%d" % c))
        x_raw = const.tile([P, NA * K], BF16, name="x_raw")
        x_src = inputs.rearrange("(p a) k -> p (a k)", a=NA)

        def load_w(c, h0, h1):
            src = weight[c * CH:(c + 1) * CH, :].rearrange("(h p b) k -> p h (b k)", h=2, b=2)
            nc.sync.dma_start(out=w_raw[c][:, 2048 * h0:2048 * h1].rearrange("p (h x) -> p h x", x=2 * K),
                              in_=src[:, h0:h1, :])

        def load_x(i):
            nc.sync.dma_start(out=x_raw[:, i * 2048:(i + 1) * 2048], in_=x_src[:, i * 2048:(i + 1) * 2048])

        load_w(0, 0, 1)
        load_x(0)
        load_w(0, 1, 2)
        load_x(1)
        load_x(2)
        load_w(1, 0, 1)
        load_x(3)
        load_w(1, 1, 2)
        bias_b = const.tile([P, N - 2 * CH], BF16, name="bias_b")
        for c in range(2, NCH):
            load_w(c, 0, 2)
            if c == 4:
                nc.sync.dma_start(out=bias_b[:], in_=bias[2 * CH:N].partition_broadcast(P))

        ident_b = const.tile([P, P], BF16, name="ident_b")
        make_identity(nc, ident_b[:])
        ident_f = const.tile([P, P], F32, name="ident_f")
        make_identity(nc, ident_f[:])
        kk_m = const.tile([P, 1], F32, name="kk_m")
        nc.vector.tensor_scalar(out=kk_m[:], in0=kk_bf[:], scalar1=KK_THRESHOLD, scalar2=BIG,
                                op0=ALU.is_ge, op1=ALU.mult)
        kk_eff = const.tile([P, 1], F32, name="kk_eff")
        nc.vector.tensor_scalar(out=kk_eff[:], in0=kk_bf[:], scalar1=kk_m[:, 0:1], scalar2=BIG,
                                op0=ALU.add, op1=ALU.min)
        nmk_f = const.tile([P, 1], F32, name="nmk_f")
        nc.vector.tensor_copy(out=nmk_f[:], in_=nmk_bf[:])

        bias_n = const.tile([P, N], F32, name="bias_n")
        xg = []
        xc = []
        xs = []
        for q in range(NA // 2):
            xg.append(const.tile([P, G, 1024], BF16, name="xg%d" % q, align_bytes=64))
            xc.append(const.tile([P, G, 256], U32, name="xc%d" % q, align_bytes=64))
            xs.append(const.tile([P, G, 256], U8, name="xs%d" % q, align_bytes=64))
        xf = x_raw[:].bitcast(F32)
        out_v = out.rearrange("(r a) n -> r a n", a=NA)

        wp_t = {}
        wg_t = {}
        wc_t = {}
        ws_t = {}
        acc_t = {}
        ost_t = {}

        def w_permute(c, eng):
            if c not in wp_t:
                wp_t[c] = wpp.tile([P, 4 * 512], F32, name="wp")
            for m in range(4):
                if PERMUTE.get(m) != eng:
                    continue
                cols = slice(512 * m, 512 * m + 512)
                dst = wp_t[c][:, cols].rearrange("p (g u w) -> p g u w", g=G, u=2)
                src = w_raw[c][:].bitcast(F32)[:, cols].rearrange("p (g w u) -> p g u w", g=G, u=2)
                if eng == "s":
                    nc.scalar.copy(out=dst, in_=src)
                elif eng == "g":
                    for g in range(G):
                        gs = slice(512 * m + 256 * g, 512 * m + 256 * g + 256)
                        nc.gpsimd.tensor_scalar(
                            out=wp_t[c][:, gs].bitcast(BF16).rearrange("p (u w e) -> p u w e", u=2, e=2),
                            in0=w_raw[c][:].bitcast(F32)[:, gs].bitcast(BF16).rearrange("p (w u e) -> p u w e", u=2, e=2),
                            scalar1=1.0, scalar2=0.0, op0=ALU.mult, op1=ALU.add)
                else:
                    nc.vector.tensor_copy(out=dst, in_=src)

        def bias_chunk(c, eng):
            bp = ps_t.tile([P, CH], F32, name="bp", tag="tp")
            nc.tensor.matmul(out=bp[:], lhsT=ident_b[:, c:c + 1].to_broadcast([P, P]), rhs=brow[:],
                             start=True, stop=True)
            dst = bias_n[:, c * CH:(c + 1) * CH]
            if eng == "v":
                nc.vector.tensor_scalar(out=dst, in0=bp[:], scalar1=nmk_f[:, 0:1], scalar2=None, op0=ALU.mult)
            else:
                nc.scalar.activation(out=dst, in_=bp[:], func=ACT.Copy, scale=nmk_f[:, 0:1])

        def bias_scale(c):
            cs = slice(c * CH, (c + 1) * CH)
            nc.gpsimd.tensor_scalar(out=bias_n[:, cs], in0=bias_b[:, (c - 2) * CH:(c - 1) * CH], scalar1=nmk_f[:, 0:1],
                                    scalar2=0.0, op0=ALU.mult, op1=ALU.add)

        def w_bank(c, g, bh):
            wg = wg_t[c]
            tp = ps_t.tile([P, 512], F32, name="tp", tag="tp")
            for m in range(4):
                blk = 2 * bh + m % 2
                col = 512 * blk + 256 * g
                u = m // 2
                if c in wp_t and blk in PERMUTE:
                    words = wp_t[c][:, col + 128 * u:col + 128 * u + 128]
                else:
                    words = w_raw[c][:].bitcast(F32)[:, col + u:col + 256:2]
                nc.tensor.transpose(tp[:, 128 * m:128 * m + 128], words, ident_f[:])
            src = tp[:].bitcast(BF16).rearrange("p (u j e) -> p j u e", u=2, j=2 * P, e=2)
            src = src.rearrange("p (b j) u e -> p b j u e", b=2)
            dst = wg[:, g, :].rearrange("p (b h j u e) -> p h b j u e", b=2, h=2, j=P, u=2, e=2)[:, bh]
            nc.scalar.activation(out=dst, in_=src, func=ACT.Tanh, scale=kk_eff[:, 0:1])

        def w_new(c):
            wg_t[c] = wgp.tile([P, G, 4 * CH], BF16, name="wg", align_bytes=64)

        def w_quant(c, g):
            if g == 0:
                wc_t[c] = wcp.tile([P, G, CH], U32, name="wc", align_bytes=64)
                ws_t[c] = wcp.tile([P, G, CH], U8, name="ws", align_bytes=64)
            nc.vector.quantize_mx(out=wc_t[c][:, g, :].bitcast(FP8X4), scales=ws_t[c][:, g, :],
                                  in_=wg_t[c][:, g, :])

        def x_transpose(a, eng="v"):
            tpx = ps_a.tile([P, 512], F32, name="tpx", tag="acc")
            for j in range(4):
                col = 512 * a + 256 * (j // 2)
                nc.tensor.transpose(tpx[:, 128 * j:128 * j + 128], xf[:, col + j % 2:col + 256:2], ident_f[:])
            r0 = 256 * (a % 2)
            dst = xg[a // 2][:].bitcast(F32)[:, :, r0:r0 + 256].rearrange("p g (r u) -> p g r u", u=2)
            src = tpx[:].rearrange("p (g u r) -> p g r u", g=G, u=2)
            if eng == "v":
                nc.vector.tensor_copy(out=dst, in_=src)
            else:
                nc.scalar.copy(out=dst, in_=src)

        def x_quant(q):
            nc.vector.quantize_mx(out=xc[q][:].rearrange("p g t -> p (g t)").bitcast(FP8X4),
                                  scales=xs[q][:].rearrange("p g t -> p (g t)"),
                                  in_=xg[q][:].rearrange("p g t -> p (g t)"))

        def mx(c, a):
            acc = ps_a.tile([P, CH], F32, name="acc", tag="acc")
            for g in range(G):
                nc.tensor.matmul_mx(out=acc[:],
                                    lhsT=xc[a // 2][:, g, P * (a % 2):P * (a % 2) + P].bitcast(FP8X4),
                                    lhsT_scale=xs[a // 2][:, g, P * (a % 2):P * (a % 2) + P],
                                    rhs=wc_t[c][:, g, :].bitcast(FP8X4),
                                    rhs_scale=ws_t[c][:, g, :],
                                    start=(g == 0), stop=(g == G - 1))
            acc_t[a] = acc

        def epilogue(c, a):
            n_st = 1 if c >= NCH - 2 else 2
            cs = slice(c * CH, (c + 1) * CH)
            if a % n_st == 0:
                ost_t[0] = osp.tile([P, 2, CH], F32, name="ost")
            ost = ost_t[0]
            nc.vector.scalar_tensor_tensor(
                out=ost[:, a % n_st, :].rearrange("q (j b) -> q j b", b=2),
                in0=acc_t[a][:].rearrange("q (b j) -> q j b", b=2), scalar=nmk_f[:, 0:1],
                in1=bias_n[:, cs].rearrange("q (j b) -> q j b", b=2), op0=ALU.mult, op1=ALU.add)
            if a % n_st == n_st - 1:
                nc.sync.dma_start(out=out_v[:, a - n_st + 1:a + 1, cs], in_=ost[:, 0:n_st, :])

        bias_chunk(0, "v")
        bias_chunk(1, "v")
        w_new(0)
        w_bank(0, 0, 0)
        w_bank(0, 1, 0)
        x_transpose(0)
        x_transpose(1)
        w_bank(0, 0, 1)
        w_bank(0, 1, 1)
        x_quant(0)
        x_transpose(2)
        w_quant(0, 0)
        x_transpose(3)
        w_quant(0, 1)
        x_quant(1)
        x_transpose(4, "s")
        x_transpose(5, "s")
        w_new(1)
        w_bank(1, 0, 0)
        w_bank(1, 1, 0)
        mx(0, 0)
        epilogue(0, 0)
        x_quant(2)
        mx(0, 1)
        epilogue(0, 1)
        x_transpose(6, "s")
        x_transpose(7, "s")
        mx(0, 2)
        epilogue(0, 2)
        x_quant(3)
        w_bank(1, 0, 1)
        w_bank(1, 1, 1)
        for a in range(3, NA):
            mx(0, a)
            epilogue(0, a)
            if a == 3:
                w_permute(2, "v")
            if a == 4:
                w_quant(1, 0)
            if a == 6:
                w_quant(1, 1)
        w_permute(2, "s")

        w_permute(2, "g")
        w_permute(3, "g")
        for c in range(1, NCH):
            n = c + 1
            if n < NCH:
                w_new(n)
                k = 0
                for g in range(G):
                    for bh in range(2):
                        w_bank(n, g, bh)
                        k += 1
                        if k == 2 and n + 1 < NCH:
                            w_permute(n + 1, "s")
            for a in range(NA):
                mx(c, a)
                if a == 3 and n < NCH:
                    bias_scale(n)
                if a == 3 and c + 3 < NCH:
                    w_permute(c + 3, "g")
                epilogue(c, a)
                if n + 1 < NCH and a == 0:
                    w_permute(n + 1, "v")
                if n < NCH and a == 2:
                    w_quant(n, 0)
                if n < NCH and a == (6 if n < NCH - 1 else 4):
                    w_quant(n, 1)
